import numpy as np
import ml_dtypes

BF16 = ml_dtypes.bfloat16


def bf(x):
    return np.asarray(x, np.float32).astype(BF16)


def f32(x):
    return np.asarray(x, np.float32)


def f64(x):
    return np.asarray(x).astype(np.float64)


def striped(idx):
    return np.tile(idx.reshape(-1, 16).T, (8, 1))


D, F, S, N = 128, 128, 512, 128
CUT = 5.0


def setup_inputs():
    return {
        "emb": f32(np.random.standard_normal((D, S))),
        "dist": f32(np.random.uniform(0.5, 7.0, (1, N))),
        "fw1": f32(0.5 * np.random.standard_normal((F, 1))),
        "fb1": f32(0.1 * np.random.standard_normal((F, 1))),
        "fw2": bf(np.random.standard_normal((F, F)) * np.sqrt(2.0 / F)),
        "fb2": f32(0.1 * np.random.standard_normal((F, 1))),
        "db1": f32(0.1 * np.random.standard_normal((D, 1))),
        "dw2": bf(np.random.standard_normal((D, D)) * np.sqrt(2.0 / D)),
        "db2": f32(0.1 * np.random.standard_normal((D, 1))),
        "offs": striped(np.random.permutation(np.tile(np.arange(S), 2))[:N]),
    }


def reference(emb, dist, fw1, fb1, fw2, fb2, db1, dw2, db2, offs):
    idx = offs[:16].T.reshape(-1)
    r = f64(dist)
    cut = np.cos(r * (np.pi / (2.0 * CUT))) * (r <= CUT)
    h = np.maximum(f64(fw1) * r + f64(fb1), 0.0)
    t = (f64(fw2).T @ h + f64(fb2)) * cut
    a = np.maximum(t + f64(db1), 0.0)
    v = f64(dw2).T @ a + f64(db2)
    return f64(emb)[:, idx] + v

@@ -1,0 +1,72 @@
+import math
+
+import concourse.mybir as mybir
+
+F32 = mybir.dt.float32
+BF16 = mybir.dt.bfloat16
+U16 = mybir.dt.uint16
+ALU = mybir.AluOpType
+FUNC = mybir.ActivationFunctionType
+
+P = 128
+TYPES = 512
+ATOMS = 128
+CUTOFF = 5.0
+
+FLOPS = 2 * (2 * P * P * ATOMS)
+
+
+def tile_schnet_kernel(tc, emb, dist, fw1, fb1, fw2, fb2, db1, dw2, db2, offs, out):
+    nc = tc.nc
+    with (
+        tc.tile_pool(name="held", bufs=1) as held,
+        tc.psum_pool(name="psum", bufs=1) as psum,
+    ):
+        r = held.tile([P, ATOMS], F32, name="r")
+        nc.sync.dma_start(r[:], dist.broadcast_to([P, ATOMS]))
+        fw1_col = held.tile([P, 1], F32, name="fw1_col")
+        nc.scalar.dma_start(fw1_col[:], fw1)
+        fb1_col = held.tile([P, 1], F32, name="fb1_col")
+        nc.sync.dma_start(fb1_col[:], fb1)
+        fw2_sb = held.tile([P, P], BF16, name="fw2_sb")
+        nc.scalar.dma_start(fw2_sb[:], fw2)
+        offsets = held.tile([P, ATOMS // 16], U16, name="offsets")
+        nc.sync.dma_start(offsets[:], offs)
+        fb2_col = held.tile([P, 1], F32, name="fb2_col")
+        nc.scalar.dma_start(fb2_col[:], fb2)
+        db1_col = held.tile([P, 1], F32, name="db1_col")
+        nc.sync.dma_start(db1_col[:], db1)
+        dw2_sb = held.tile([P, P], BF16, name="dw2_sb")
+        nc.scalar.dma_start(dw2_sb[:], dw2)
+        db2_col = held.tile([P, 1], F32, name="db2_col")
+        nc.sync.dma_start(db2_col[:], db2)
+        table = held.tile([P, TYPES], F32, name="table")
+        nc.gpsimd.dma_start(table[:], emb)
+
+        h = held.tile([P, ATOMS], BF16, name="h")
+        nc.scalar.activation(h[:], r[:], FUNC.Relu, bias=fb1_col[:], scale=fw1_col[:])
+
+        r_clamped = held.tile([P, ATOMS], F32, name="r_clamped")
+        nc.vector.tensor_scalar_min(r_clamped[:], r[:], CUTOFF)
+        quarter_turn = held.tile([P, 1], F32, name="quarter_turn")
+        nc.vector.memset(quarter_turn[:], math.pi / 2.0)
+        cut = held.tile([P, ATOMS], F32, name="cut")
+        nc.scalar.activation(
+            cut[:], r_clamped[:], FUNC.Sin, bias=quarter_turn[:], scale=-math.pi / (2.0 * CUTOFF)
+        )
+
+        filter_psum = psum.tile([P, ATOMS], F32, name="filter_psum")
+        nc.tensor.matmul(filter_psum[:], fw2_sb[:], h[:], start=True, stop=True)
+        t = held.tile([P, ATOMS], F32, name="t")
+        nc.vector.scalar_tensor_tensor(t[:], filter_psum[:], fb2_col[:], cut[:], ALU.add, ALU.mult)
+        a = held.tile([P, ATOMS], BF16, name="a")
+        nc.vector.tensor_scalar(a[:], t[:], db1_col[:], 0.0, ALU.add, ALU.max)
+
+        dense_psum = psum.tile([P, ATOMS], F32, name="dense_psum")
+        nc.tensor.matmul(dense_psum[:], dw2_sb[:], a[:], start=True, stop=True)
+        v = held.tile([P, ATOMS], F32, name="v")
+        nc.vector.tensor_scalar_add(v[:], dense_psum[:], db2_col[:])
+
+        result = held.tile([P, ATOMS], F32, name="result")
+        nc.vector.tensor_tensor(result[:], table[:].indirect(offsets[:]), v[:], ALU.add)
+        nc.sync.dma_start(out, result[:])

@@ -29,17 +29,17 @@ def tile_schnet_kernel(tc, emb, dist, fw1, fb1, fw2, fb2, db1, dw2, db2, offs, o
         fb1_col = held.tile([P, 1], F32, name="fb1_col")
         nc.sync.dma_start(fb1_col[:], fb1)
         fw2_sb = held.tile([P, P], BF16, name="fw2_sb")
-        nc.scalar.dma_start(fw2_sb[:], fw2)
-        offsets = held.tile([P, ATOMS // 16], U16, name="offsets")
-        nc.sync.dma_start(offsets[:], offs)
+        nc.sync.dma_start(fw2_sb[:], fw2)
         fb2_col = held.tile([P, 1], F32, name="fb2_col")
-        nc.scalar.dma_start(fb2_col[:], fb2)
+        nc.sync.dma_start(fb2_col[:], fb2)
         db1_col = held.tile([P, 1], F32, name="db1_col")
         nc.sync.dma_start(db1_col[:], db1)
         dw2_sb = held.tile([P, P], BF16, name="dw2_sb")
-        nc.scalar.dma_start(dw2_sb[:], dw2)
+        nc.sync.dma_start(dw2_sb[:], dw2)
         db2_col = held.tile([P, 1], F32, name="db2_col")
         nc.sync.dma_start(db2_col[:], db2)
+        offsets = held.tile([P, ATOMS // 16], U16, name="offsets")
+        nc.sync.dma_start(offsets[:], offs)
         table = held.tile([P, TYPES], F32, name="table")
         nc.gpsimd.dma_start(table[:], emb)
 

@@ -12,6 +12,7 @@ P = 128
 TYPES = 512
 ATOMS = 128
 CUTOFF = 5.0
+HALF = ATOMS // 2
 
 FLOPS = 2 * (2 * P * P * ATOMS)
 
@@ -29,22 +30,26 @@ def tile_schnet_kernel(tc, emb, dist, fw1, fb1, fw2, fb2, db1, dw2, db2, offs, o
         fb1_col = held.tile([P, 1], F32, name="fb1_col")
         nc.sync.dma_start(fb1_col[:], fb1)
         fw2_sb = held.tile([P, P], BF16, name="fw2_sb")
-        nc.sync.dma_start(fw2_sb[:], fw2)
+        nc.scalar.dma_start(fw2_sb[:], fw2)
+        offsets = held.tile([P, ATOMS // 16], U16, name="offsets")
+        nc.sync.dma_start(offsets[:], offs)
         fb2_col = held.tile([P, 1], F32, name="fb2_col")
-        nc.sync.dma_start(fb2_col[:], fb2)
+        nc.scalar.dma_start(fb2_col[:], fb2)
         db1_col = held.tile([P, 1], F32, name="db1_col")
         nc.sync.dma_start(db1_col[:], db1)
         dw2_sb = held.tile([P, P], BF16, name="dw2_sb")
-        nc.sync.dma_start(dw2_sb[:], dw2)
+        nc.scalar.dma_start(dw2_sb[:], dw2)
         db2_col = held.tile([P, 1], F32, name="db2_col")
         nc.sync.dma_start(db2_col[:], db2)
-        offsets = held.tile([P, ATOMS // 16], U16, name="offsets")
-        nc.sync.dma_start(offsets[:], offs)
         table = held.tile([P, TYPES], F32, name="table")
         nc.gpsimd.dma_start(table[:], emb)
 
+
+        halves = [slice(0, HALF), slice(HALF, ATOMS)]
+
         h = held.tile([P, ATOMS], BF16, name="h")
-        nc.scalar.activation(h[:], r[:], FUNC.Relu, bias=fb1_col[:], scale=fw1_col[:])
+        for cols in halves:
+            nc.scalar.activation(h[:, cols], r[:, cols], FUNC.Relu, bias=fb1_col[:], scale=fw1_col[:])
 
         r_clamped = held.tile([P, ATOMS], F32, name="r_clamped")
         nc.vector.tensor_scalar_min(r_clamped[:], r[:], CUTOFF)
@@ -55,18 +60,27 @@ def tile_schnet_kernel(tc, emb, dist, fw1, fb1, fw2, fb2, db1, dw2, db2, offs, o
             cut[:], r_clamped[:], FUNC.Sin, bias=quarter_turn[:], scale=-math.pi / (2.0 * CUTOFF)
         )
 
-        filter_psum = psum.tile([P, ATOMS], F32, name="filter_psum")
-        nc.tensor.matmul(filter_psum[:], fw2_sb[:], h[:], start=True, stop=True)
+        filter_psum = [psum.tile([P, HALF], F32, name=f"filter_psum{i}") for i in range(2)]
+        for i, cols in enumerate(halves):
+            nc.tensor.matmul(filter_psum[i][:], fw2_sb[:], h[:, cols], start=True, stop=True)
         t = held.tile([P, ATOMS], F32, name="t")
-        nc.vector.scalar_tensor_tensor(t[:], filter_psum[:], fb2_col[:], cut[:], ALU.add, ALU.mult)
+        for i, cols in enumerate(halves):
+            nc.vector.scalar_tensor_tensor(
+                t[:, cols], filter_psum[i][:], fb2_col[:], cut[:, cols], ALU.add, ALU.mult
+            )
         a = held.tile([P, ATOMS], BF16, name="a")
-        nc.vector.tensor_scalar(a[:], t[:], db1_col[:], 0.0, ALU.add, ALU.max)
+        for cols in halves:
+            nc.vector.tensor_scalar(a[:, cols], t[:, cols], db1_col[:], 0.0, ALU.add, ALU.max)
 
-        dense_psum = psum.tile([P, ATOMS], F32, name="dense_psum")
-        nc.tensor.matmul(dense_psum[:], dw2_sb[:], a[:], start=True, stop=True)
+        dense_psum = [psum.tile([P, HALF], F32, name=f"dense_psum{i}") for i in range(2)]
+        for i, cols in enumerate(halves):
+            nc.tensor.matmul(dense_psum[i][:], dw2_sb[:], a[:, cols], start=True, stop=True)
         v = held.tile([P, ATOMS], F32, name="v")
-        nc.vector.tensor_scalar_add(v[:], dense_psum[:], db2_col[:])
+        for i, cols in enumerate(halves):
+            nc.vector.tensor_scalar_add(v[:, cols], dense_psum[i][:], db2_col[:])
 
         result = held.tile([P, ATOMS], F32, name="result")
-        nc.vector.tensor_tensor(result[:], table[:].indirect(offsets[:]), v[:], ALU.add)
+        for i, cols in enumerate(halves):
+            piece = offsets[:, i * (HALF // 16) : (i + 1) * (HALF // 16)]
+            nc.vector.tensor_tensor(result[:, cols], table[:].indirect(piece), v[:, cols], ALU.add)
         nc.sync.dma_start(out, result[:])

@@ -12,6 +12,7 @@ P = 128
 TYPES = 512
 ATOMS = 128
 CUTOFF = 5.0
+QUARTER = ATOMS // 4
 HALF = ATOMS // 2
 
 FLOPS = 2 * (2 * P * P * ATOMS)
@@ -45,10 +46,10 @@ def tile_schnet_kernel(tc, emb, dist, fw1, fb1, fw2, fb2, db1, dw2, db2, offs, o
         nc.gpsimd.dma_start(table[:], emb)
 
 
-        halves = [slice(0, HALF), slice(HALF, ATOMS)]
+        quarters = [slice(q * QUARTER, (q + 1) * QUARTER) for q in range(4)]
 
         h = held.tile([P, ATOMS], BF16, name="h")
-        for cols in halves:
+        for cols in quarters:
             nc.scalar.activation(h[:, cols], r[:, cols], FUNC.Relu, bias=fb1_col[:], scale=fw1_col[:])
 
         r_clamped = held.tile([P, ATOMS], F32, name="r_clamped")
@@ -60,27 +61,28 @@ def tile_schnet_kernel(tc, emb, dist, fw1, fb1, fw2, fb2, db1, dw2, db2, offs, o
             cut[:], r_clamped[:], FUNC.Sin, bias=quarter_turn[:], scale=-math.pi / (2.0 * CUTOFF)
         )
 
-        filter_psum = [psum.tile([P, HALF], F32, name=f"filter_psum{i}") for i in range(2)]
-        for i, cols in enumerate(halves):
-            nc.tensor.matmul(filter_psum[i][:], fw2_sb[:], h[:, cols], start=True, stop=True)
+        filter_psum = [psum.tile([P, QUARTER], F32, name=f"filter_psum{q}") for q in range(4)]
+        for q, cols in enumerate(quarters):
+            nc.tensor.matmul(filter_psum[q][:], fw2_sb[:], h[:, cols], start=True, stop=True)
         t = held.tile([P, ATOMS], F32, name="t")
-        for i, cols in enumerate(halves):
-            nc.vector.scalar_tensor_tensor(
-                t[:, cols], filter_psum[i][:], fb2_col[:], cut[:, cols], ALU.add, ALU.mult
-            )
         a = held.tile([P, ATOMS], BF16, name="a")
-        for cols in halves:
+        for q, cols in enumerate(quarters):
+            nc.vector.scalar_tensor_tensor(
+                t[:, cols], filter_psum[q][:], fb2_col[:], cut[:, cols], ALU.add, ALU.mult
+            )
+        for cols in quarters:
             nc.vector.tensor_scalar(a[:, cols], t[:, cols], db1_col[:], 0.0, ALU.add, ALU.max)
 
-        dense_psum = [psum.tile([P, HALF], F32, name=f"dense_psum{i}") for i in range(2)]
-        for i, cols in enumerate(halves):
-            nc.tensor.matmul(dense_psum[i][:], dw2_sb[:], a[:, cols], start=True, stop=True)
+        dense_psum = [psum.tile([P, QUARTER], F32, name=f"dense_psum{q}") for q in range(4)]
+        for q, cols in enumerate(quarters):
+            nc.tensor.matmul(dense_psum[q][:], dw2_sb[:], a[:, cols], start=True, stop=True)
         v = held.tile([P, ATOMS], F32, name="v")
-        for i, cols in enumerate(halves):
-            nc.vector.tensor_scalar_add(v[:, cols], dense_psum[i][:], db2_col[:])
+        for q, cols in enumerate(quarters):
+            nc.vector.tensor_scalar_add(v[:, cols], dense_psum[q][:], db2_col[:])
 
         result = held.tile([P, ATOMS], F32, name="result")
-        for i, cols in enumerate(halves):
+        for i in range(2):
+            cols = slice(i * HALF, (i + 1) * HALF)
             piece = offsets[:, i * (HALF // 16) : (i + 1) * (HALF // 16)]
             nc.vector.tensor_tensor(result[:, cols], table[:].indirect(piece), v[:, cols], ALU.add)
         nc.sync.dma_start(out, result[:])

import math

import concourse.mybir as mybir

F32 = mybir.dt.float32
BF16 = mybir.dt.bfloat16
U16 = mybir.dt.uint16
ALU = mybir.AluOpType
FUNC = mybir.ActivationFunctionType

P = 128
TYPES = 512
ATOMS = 128
CUTOFF = 5.0
QUARTER = ATOMS // 4
HALF = ATOMS // 2

FLOPS = 2 * (2 * P * P * ATOMS)


def tile_schnet_kernel(tc, emb, dist, fw1, fb1, fw2, fb2, db1, dw2, db2, offs, out):
    nc = tc.nc
    with (
        tc.tile_pool(name="held", bufs=1) as held,
        tc.psum_pool(name="psum", bufs=1) as psum,
    ):
        r = held.tile([P, ATOMS], F32, name="r")
        nc.sync.dma_start(r[:], dist.broadcast_to([P, ATOMS]))
        fw1_col = held.tile([P, 1], F32, name="fw1_col")
        nc.scalar.dma_start(fw1_col[:], fw1)
        fb1_col = held.tile([P, 1], F32, name="fb1_col")
        nc.sync.dma_start(fb1_col[:], fb1)
        fw2_sb = held.tile([P, P], BF16, name="fw2_sb")
        nc.scalar.dma_start(fw2_sb[:], fw2)
        offsets = held.tile([P, ATOMS // 16], U16, name="offsets")
        nc.sync.dma_start(offsets[:], offs)
        fb2_col = held.tile([P, 1], F32, name="fb2_col")
        nc.scalar.dma_start(fb2_col[:], fb2)
        db1_col = held.tile([P, 1], F32, name="db1_col")
        nc.sync.dma_start(db1_col[:], db1)
        dw2_sb = held.tile([P, P], BF16, name="dw2_sb")
        nc.scalar.dma_start(dw2_sb[:], dw2)
        db2_col = held.tile([P, 1], F32, name="db2_col")
        nc.sync.dma_start(db2_col[:], db2)
        table = held.tile([P, TYPES], F32, name="table")
        nc.gpsimd.dma_start(table[:], emb)


        quarters = [slice(q * QUARTER, (q + 1) * QUARTER) for q in range(4)]

        h = held.tile([P, ATOMS], BF16, name="h")
        for cols in quarters:
            nc.scalar.activation(h[:, cols], r[:, cols], FUNC.Relu, bias=fb1_col[:], scale=fw1_col[:])

        r_clamped = held.tile([P, ATOMS], F32, name="r_clamped")
        nc.vector.tensor_scalar_min(r_clamped[:], r[:], CUTOFF)
        quarter_turn = held.tile([P, 1], F32, name="quarter_turn")
        nc.vector.memset(quarter_turn[:], math.pi / 2.0)
        cut = held.tile([P, ATOMS], F32, name="cut")
        nc.scalar.activation(
            cut[:], r_clamped[:], FUNC.Sin, bias=quarter_turn[:], scale=-math.pi / (2.0 * CUTOFF)
        )

        filter_psum = [psum.tile([P, QUARTER], F32, name=f"filter_psum{q}") for q in range(4)]
        for q, cols in enumerate(quarters):
            nc.tensor.matmul(filter_psum[q][:], fw2_sb[:], h[:, cols], start=True, stop=True)
        t = held.tile([P, ATOMS], F32, name="t")
        a = held.tile([P, ATOMS], BF16, name="a")
        for q, cols in enumerate(quarters):
            nc.vector.scalar_tensor_tensor(
                t[:, cols], filter_psum[q][:], fb2_col[:], cut[:, cols], ALU.add, ALU.mult
            )
        for cols in quarters:
            nc.vector.tensor_scalar(a[:, cols], t[:, cols], db1_col[:], 0.0, ALU.add, ALU.max)

        dense_psum = [psum.tile([P, QUARTER], F32, name=f"dense_psum{q}") for q in range(4)]
        for q, cols in enumerate(quarters):
            nc.tensor.matmul(dense_psum[q][:], dw2_sb[:], a[:, cols], start=True, stop=True)
        v = held.tile([P, ATOMS], F32, name="v")
        for q, cols in enumerate(quarters):
            nc.vector.tensor_scalar_add(v[:, cols], dense_psum[q][:], db2_col[:])

        result = held.tile([P, ATOMS], F32, name="result")
        for i in range(2):
            cols = slice(i * HALF, (i + 1) * HALF)
            piece = offsets[:, i * (HALF // 16) : (i + 1) * (HALF // 16)]
            nc.vector.tensor_tensor(result[:, cols], table[:].indirect(piece), v[:, cols], ALU.add)
        nc.sync.dma_start(out, result[:])
